import numpy as np
import ml_dtypes


def mxq(x, axis, fmt="e4m3"):
    dtype, down = {"e4m3": (ml_dtypes.float8_e4m3fn, 7), "e5m2": (ml_dtypes.float8_e5m2, 14)}[fmt]
    v = np.moveaxis(np.asarray(x, np.float32).astype(ml_dtypes.bfloat16).astype(np.float64), axis, -1)
    blocks = v.reshape(v.shape[:-1] + (-1, 32))
    amax = np.abs(blocks).max(-1, keepdims=True)
    byte = np.maximum(np.where(amax > 0, np.frexp(amax)[1] - 1 + 127, 0) - down, 1)
    scale = np.exp2(byte - 127.0)
    codes = (blocks / scale).astype(np.float32).astype(dtype).astype(np.float64)
    return np.moveaxis((codes * scale).reshape(v.shape), -1, axis)


WIDE = False


def mx_kscale(k):
    if not WIDE:
        return np.ones(k)
    levels = np.array([10, -10, 5, -5, 0])
    if k % 512:
        return np.exp2(np.random.permutation(np.resize(levels, k // 32))).repeat(32)
    a = np.empty((k // 512, 16))
    for p in range(k // 512):
        a[p, :8] = np.random.permutation(np.resize(levels, 8))
        for g in range(8):
            far = levels[np.abs(levels - a[p, g]) >= 10]
            a[p, g + 8] = far[np.random.randint(len(far))]
    return np.exp2(a.ravel()).repeat(32)


BF16 = ml_dtypes.bfloat16


def bf(x):
    return np.asarray(x, np.float32).astype(BF16)


def f64(x):
    return np.asarray(x).astype(np.float64)


B, T, S, Dt, Df = 2, 512, 512, 2048, 2048
EPS = 1e-6


def rmsnorm(x, w):
    return x * (1.0 / np.sqrt(np.mean(x * x, axis=-1, keepdims=True) + EPS)) * w


def setup_inputs():
    s = mx_kscale(Dt)
    t = mx_kscale(Df)
    return {"text": bf(np.random.standard_normal((B, T, Dt)) * s),
            "Wq_w": bf(np.random.standard_normal((Df, Dt)) / np.sqrt(Dt) / s[None, :]),
            "Wq_b": bf(np.random.standard_normal(Df) * 0.3),
            "qn_w": bf((1.0 + 0.1 * np.random.standard_normal(Df)) * t),
            "k_norm": bf(np.random.standard_normal((B, S, Df)) / t)}


def reference(text, Wq_w, Wq_b, qn_w, k_norm):
    q = (mxq(f64(text), 2, "e4m3") @ mxq(f64(Wq_w), 1, "e4m3").T) + f64(Wq_b)
    q = rmsnorm(q, f64(qn_w))
    scale = 1.0 / np.sqrt(Df)
    return (mxq(q, 2, "e4m3") @ mxq(f64(k_norm), 2, "e4m3").transpose(0, 2, 1)) * scale

@@ -1,0 +1,292 @@
+from contextlib import ExitStack
+
+import concourse.mybir as mybir
+from concourse.masks import make_identity
+
+F32 = mybir.dt.float32
+BF16 = mybir.dt.bfloat16
+U32 = mybir.dt.uint32
+U8 = mybir.dt.uint8
+FP8X4 = mybir.dt.float8_e4m3fn_x4
+ACT = mybir.ActivationFunctionType
+ALU = mybir.AluOpType
+
+P = 128
+D = 2048
+PASSES = 4
+TOKENS = 1024
+BLOCK = 512
+UNIT_ROWS = 256
+W_UNITS = D // UNIT_ROWS
+EPS = 1e-6
+SCORE_SCALE = 1.0 / (2048.0 ** 0.5)
+
+FLOPS = 2 * TOKENS * D * D + 2 * TOKENS * BLOCK * D
+
+RAW_BUFS = 4
+LEAD = 4
+
+
+def tile_crossattention_pb_kernel(tc, text, Wq_w, Wq_b, qn_w, k_norm, out):
+    nc = tc.nc
+    text_rows = text.flatten_outer_dims()
+    key_rows = k_norm.flatten_outer_dims()
+    out_rows = out.flatten_outer_dims()
+
+    units = [("text", 0), ("text", 1)]
+    units += [("weights", m) for m in range(W_UNITS)]
+    units += [("text", 2), ("text", 3)]
+    units += [("keys", h) for h in range(4)]
+    FIRST_KEYS = len(units) - 4
+
+    with ExitStack() as ctx:
+        consts = ctx.enter_context(tc.tile_pool(name="consts", bufs=1))
+        codes = ctx.enter_context(tc.tile_pool(name="codes", bufs=1))
+        raw_pool = ctx.enter_context(tc.tile_pool(name="raw", bufs=RAW_BUFS))
+        grouped_pool = ctx.enter_context(tc.tile_pool(name="grouped", bufs=3))
+        y_pool = ctx.enter_context(tc.tile_pool(name="y", bufs=5))
+        q_pool = ctx.enter_context(tc.tile_pool(name="q", bufs=2))
+        sq_pool = ctx.enter_context(tc.tile_pool(name="sq", bufs=3))
+        norm_pool = ctx.enter_context(tc.tile_pool(name="norm", bufs=2))
+        o_pool = ctx.enter_context(tc.tile_pool(name="o", bufs=3))
+        psum = ctx.enter_context(tc.psum_pool(name="psum", bufs=4))
+
+        def load_unit(n):
+            kind, index = units[n]
+            rows = slice(index * UNIT_ROWS, (index + 1) * UNIT_ROWS)
+            raw = raw_pool.tile([P, 2 * D], BF16, name="raw")
+            if kind == "weights":
+                group = slice((index // 2) * 512, (index // 2 + 1) * 512)
+                view = Wq_w[group, :].rearrange("(p h e) k -> p h e k", h=2, e=2)[:, index % 2]
+            elif kind == "text":
+                view = text_rows[rows, :].rearrange("(e p) k -> p e k", e=2)
+            else:
+                view = key_rows[rows, :].rearrange("(e p) k -> p e k", e=2)
+            nc.sync.dma_start(out=raw[:].rearrange("p (e k) -> p e k", e=2), in_=view)
+            return raw
+
+        vec_rows = consts.tile([P, 4 * P], BF16, name="vec_rows")
+        nc.vector.memset(vec_rows[:], 0.0)
+        nc.scalar.dma_start(out=vec_rows[0:4, :], in_=Wq_b.rearrange("(g c) -> g c", g=4))
+        nc.scalar.dma_start(out=vec_rows[4:8, :], in_=qn_w.rearrange("(g c) -> g c", g=4))
+
+        raw_of = {}
+        for n in range(RAW_BUFS):
+            raw_of[n] = load_unit(n)
+
+        ident = consts.tile([P, P], F32, name="ident")
+        make_identity(nc, ident[:])
+        mean_w = consts.tile([P, P], F32, name="mean_w")
+        nc.vector.memset(mean_w[:], 1.0 / D)
+        eps = consts.tile([P, 1], F32, name="eps")
+        nc.vector.memset(eps[:], EPS)
+        warm = consts.tile([P, 1], F32, name="warm")
+        nc.scalar.activation(out=warm[:], in_=eps[:], func=ACT.Abs_reciprocal_sqrt)
+
+        bias_gain = consts.tile([P, 32], F32, name="bias_gain")
+        bias = bias_gain[:, 0:16]
+        gain = bias_gain[:, 16:32]
+        gain_bias = consts.tile([P, 16], F32, name="gain_bias")
+
+        def spread_bias_and_gain():
+            vec_bank = psum.tile([P, 2, 2, P], F32, name="tp")
+            vec_words = vec_rows[:].bitcast(F32).rearrange("p (c u) -> p c u", u=2)
+            for u in range(2):
+                nc.tensor.transpose(vec_bank[:, 0, u, :], vec_words[:, :, u], ident[:])
+            nc.vector.tensor_copy(
+                out=bias_gain[:].rearrange("p (r u v) -> p r u v", u=2, v=2),
+                in_=vec_bank[:, 0, :, 0:8].bitcast(BF16).rearrange("p u (r v) -> p r u v", v=2),
+            )
+            nc.vector.tensor_tensor(out=gain_bias[:], in0=gain, in1=bias, op=ALU.mult)
+
+        w_codes = []
+        w_scales = []
+        for m in range(W_UNITS):
+            w_codes.append(codes.tile([P, 2 * PASSES * P], U32, name="w_codes%d" % m, align_bytes=64))
+            w_scales.append(codes.tile([P, 2 * PASSES * P], U8, name="w_scales%d" % m, align_bytes=64))
+        text_codes = codes.tile([P, PASSES, TOKENS], U32, name="text_codes", align_bytes=64)
+        text_scales = codes.tile([P, PASSES, TOKENS], U8, name="text_scales", align_bytes=64)
+        key_codes = codes.tile([P, PASSES, TOKENS], U32, name="key_codes", align_bytes=64)
+        key_scales = codes.tile([P, PASSES, TOKENS], U8, name="key_scales", align_bytes=64)
+        q_codes = codes.tile([P, PASSES, TOKENS], U32, name="q_codes", align_bytes=64)
+        q_scales = codes.tile([P, PASSES, TOKENS], U8, name="q_scales", align_bytes=64)
+
+        def transpose_unit(n):
+            kind, index = units[n]
+            words = raw_of[n][:].bitcast(F32).rearrange(
+                "p (e g c u) -> p e g c u", e=2, g=PASSES, u=2
+            )
+            grouped = grouped_pool.tile([P, 2 * D], BF16, name="grouped", align_bytes=64)
+            grouped_words = grouped[:].bitcast(F32).rearrange(
+                "p (a x r u) -> p a x r u", a=4, x=2, u=2
+            )
+            for a in range(4):
+                bank = psum.tile([P, 2, 2, P], F32, name="tp")
+                for x in range(2):
+                    if kind == "weights":
+                        e, g = a // 2, 2 * (a % 2) + x
+                    else:
+                        e, g = x, a
+                    for u in range(2):
+                        nc.tensor.transpose(bank[:, x, u, :], words[:, e, g, :, u], ident[:])
+                nc.scalar.copy(
+                    out=grouped_words[:, a], in_=bank[:].rearrange("p x u r -> p x r u")
+                )
+            return grouped
+
+        def quantise_unit(n, grouped):
+            kind, index = units[n]
+            if kind == "weights":
+                nc.vector.quantize_mx(
+                    out=w_codes[index][:].bitcast(FP8X4), scales=w_scales[index][:], in_=grouped[:]
+                )
+                return
+            dst_codes, dst_scales = (text_codes, text_scales) if kind == "text" else (key_codes, key_scales)
+            cols = slice(index * UNIT_ROWS, (index + 1) * UNIT_ROWS)
+            for g in range(PASSES):
+                nc.vector.quantize_mx(
+                    out=dst_codes[:, g, cols].bitcast(FP8X4),
+                    scales=dst_scales[:, g, cols],
+                    in_=grouped[:, g * 4 * UNIT_ROWS : (g + 1) * 4 * UNIT_ROWS],
+                )
+
+        y_of = {}
+        acc_of = {}
+        inv_of = {}
+
+        def project(block, m):
+            tokens = slice(block * BLOCK, (block + 1) * BLOCK)
+            for e in range(2):
+                j = 2 * m + e
+                bank = psum.tile([P, BLOCK], F32, name="mm")
+                for g in range(PASSES):
+                    cols = slice((PASSES * e + g) * P, (PASSES * e + g + 1) * P)
+                    nc.tensor.matmul_mx(
+                        out=bank[:],
+                        lhsT=w_codes[m][:, cols].bitcast(FP8X4),
+                        lhsT_scale=w_scales[m][:, cols],
+                        rhs=text_codes[:, g, tokens].bitcast(FP8X4),
+                        rhs_scale=text_scales[:, g, tokens],
+                        start=(g == 0),
+                        stop=(g == PASSES - 1),
+                    )
+                if j % 4 == 0:
+                    y_of[(block, j // 4)] = y_pool.tile([P, 4, BLOCK], F32, name="y4")
+                y4 = y_of[(block, j // 4)]
+                if j == 0:
+                    acc_of[block] = norm_pool.tile([P, BLOCK], F32, name="acc")
+                    sq = acc_of[block]
+                else:
+                    sq = sq_pool.tile([P, BLOCK], F32, name="sq")
+                nc.scalar.activation(
+                    out=sq[:], in_=bank[:], func=ACT.Square, bias=bias[:, j : j + 1], scale=1.0
+                )
+                if block == 0:
+                    nc.vector.tensor_scalar(
+                        out=y4[:, j % 4, :],
+                        in0=bank[:],
+                        scalar1=gain[:, j : j + 1],
+                        scalar2=gain_bias[:, j : j + 1],
+                        op0=ALU.mult,
+                        op1=ALU.add,
+                    )
+                else:
+                    nc.scalar.activation(
+                        out=y4[:, j % 4, :],
+                        in_=bank[:],
+                        func=ACT.Identity,
+                        bias=gain_bias[:, j : j + 1],
+                        scale=gain[:, j : j + 1],
+                    )
+                if j > 0:
+                    acc = acc_of[block]
+                    nc.vector.tensor_tensor(out=acc[:], in0=acc[:], in1=sq[:], op=ALU.add)
+
+        def rms_factor(block):
+            bank = psum.tile([P, BLOCK], F32, name="mm")
+            nc.tensor.matmul(out=bank[:], lhsT=mean_w[:], rhs=acc_of[block][:], start=True, stop=True)
+            inv = norm_pool.tile([P, BLOCK], F32, name="inv")
+            nc.scalar.activation(
+                out=inv[:], in_=bank[:], func=ACT.Abs_reciprocal_sqrt, bias=eps[:, 0:1], scale=1.0
+            )
+            inv_of[block] = inv
+
+        def normalise(block, g):
+            tokens = slice(block * BLOCK, (block + 1) * BLOCK)
+            q_grouped = q_pool.tile([P, 4 * BLOCK], BF16, name="q_grouped", align_bytes=64)
+            nc.vector.tensor_tensor(
+                out=q_grouped[:].rearrange("p (c i t) -> p c t i", i=4, t=4),
+                in0=y_of[(block, g)][:].rearrange("p t (c i) -> p c t i", i=4),
+                in1=inv_of[block][:]
+                .rearrange("p (c i) -> p c i", i=4)
+                .unsqueeze(2)
+                .to_broadcast([P, BLOCK // 4, 4, 4]),
+                op=ALU.mult,
+            )
+            nc.vector.quantize_mx(
+                out=q_codes[:, g, tokens].bitcast(FP8X4),
+                scales=q_scales[:, g, tokens],
+                in_=q_grouped[:],
+            )
+
+        def score_pass(block, g, banks):
+            keys = slice(block * BLOCK, (block + 1) * BLOCK)
+            for i in range(4):
+                tokens = slice(block * BLOCK + i * P, block * BLOCK + (i + 1) * P)
+                nc.tensor.matmul_mx(
+                    out=banks[i][:],
+                    lhsT=q_codes[:, g, tokens].bitcast(FP8X4),
+                    lhsT_scale=q_scales[:, g, tokens],
+                    rhs=key_codes[:, g, keys].bitcast(FP8X4),
+                    rhs_scale=key_scales[:, g, keys],
+                    start=(g == 0),
+                    stop=(g == PASSES - 1),
+                )
+
+        def store_scores(block, banks):
+            for i in range(4):
+                o_sb = o_pool.tile([P, BLOCK], F32, name="o_sb")
+                if block == 1 and i % 2 == 1:
+                    nc.vector.tensor_scalar_mul(out=o_sb[:], in0=banks[i][:], scalar1=SCORE_SCALE)
+                else:
+                    nc.scalar.activation(
+                        out=o_sb[:], in_=banks[i][:], func=ACT.Copy, scale=SCORE_SCALE
+                    )
+                rows = slice(block * BLOCK + i * P, block * BLOCK + (i + 1) * P)
+                nc.sync.dma_start(out=out_rows[rows, :], in_=o_sb[:])
+
+        grouped_of = {}
+        for n in range(2 * W_UNITS + LEAD):
+            if 1 <= n <= FIRST_KEYS and units[n - 1][0] == "weights":
+                quantise_unit(n - 1, grouped_of[n - 1])
+            if n < FIRST_KEYS:
+                grouped_of[n] = transpose_unit(n)
+                raw_of[n + RAW_BUFS] = load_unit(n + RAW_BUFS)
+                if units[n][0] == "text":
+                    quantise_unit(n, grouped_of[n])
+            if n == 1:
+                spread_bias_and_gain()
+            if n >= LEAD:
+                block, m = divmod(n - LEAD, W_UNITS)
+                project(block, m)
+                if block == 1 and m == 0:
+                    rms_factor(0)
+                if block == 1 and m % 2 == 0:
+                    normalise(0, m // 2)
+
+        grouped_of[FIRST_KEYS] = transpose_unit(FIRST_KEYS)
+        rms_factor(1)
+        for g in range(PASSES):
+            if g + 1 < 4:
+                grouped_of[FIRST_KEYS + g + 1] = transpose_unit(FIRST_KEYS + g + 1)
+            quantise_unit(FIRST_KEYS + g, grouped_of[FIRST_KEYS + g])
+            if g == 2:
+                banks0 = [psum.tile([P, BLOCK], F32, name="sc%d" % i, tag="mm") for i in range(4)]
+                for gg in range(PASSES):
+                    score_pass(0, gg, banks0)
+                store_scores(0, banks0)
+            normalise(1, g)
+        banks1 = [psum.tile([P, BLOCK], F32, name="sd%d" % i, tag="tp") for i in range(4)]
+        for g in range(PASSES):
+            score_pass(1, g, banks1)
+        store_scores(1, banks1)

@@ -24,6 +24,7 @@ SCORE_SCALE = 1.0 / (2048.0 ** 0.5)
 FLOPS = 2 * TOKENS * D * D + 2 * TOKENS * BLOCK * D
 
 RAW_BUFS = 4
+FIRST_PIECES = 4
 LEAD = 4
 
 
@@ -48,7 +49,7 @@ def tile_crossattention_pb_kernel(tc, text, Wq_w, Wq_b, qn_w, k_norm, out):
         q_pool = ctx.enter_context(tc.tile_pool(name="q", bufs=2))
         sq_pool = ctx.enter_context(tc.tile_pool(name="sq", bufs=3))
         norm_pool = ctx.enter_context(tc.tile_pool(name="norm", bufs=2))
-        o_pool = ctx.enter_context(tc.tile_pool(name="o", bufs=3))
+        o_pool = ctx.enter_context(tc.tile_pool(name="o", bufs=6))
         psum = ctx.enter_context(tc.psum_pool(name="psum", bufs=4))
 
         def load_unit(n):
@@ -62,7 +63,11 @@ def tile_crossattention_pb_kernel(tc, text, Wq_w, Wq_b, qn_w, k_norm, out):
                 view = text_rows[rows, :].rearrange("(e p) k -> p e k", e=2)
             else:
                 view = key_rows[rows, :].rearrange("(e p) k -> p e k", e=2)
-            nc.sync.dma_start(out=raw[:].rearrange("p (e k) -> p e k", e=2), in_=view)
+            raw_rows = raw[:].rearrange("p (e k) -> p e k", e=2)
+            pieces = FIRST_PIECES if n == 0 else 1
+            for c in range(pieces):
+                cols = slice(c * D // pieces, (c + 1) * D // pieces)
+                nc.sync.dma_start(out=raw_rows[:, :, cols], in_=view[:, :, cols])
             return raw
 
         vec_rows = consts.tile([P, 4 * P], BF16, name="vec_rows")

@@ -15,15 +15,17 @@ P = 128
 D = 2048
 PASSES = 4
 TOKENS = 1024
-BLOCK = 512
+BATCH = 512
 UNIT_ROWS = 256
 W_UNITS = D // UNIT_ROWS
 EPS = 1e-6
 SCORE_SCALE = 1.0 / (2048.0 ** 0.5)
 
-FLOPS = 2 * TOKENS * D * D + 2 * TOKENS * BLOCK * D
+FLOPS = 2 * TOKENS * D * D + 2 * TOKENS * BATCH * D
 
-RAW_BUFS = 4
+BLOCKS = ((0, 512), (512, 256), (768, 256))
+
+RAW_BUFS = 3
 FIRST_PIECES = 4
 LEAD = 4
 
@@ -38,18 +40,20 @@ def tile_crossattention_pb_kernel(tc, text, Wq_w, Wq_b, qn_w, k_norm, out):
     units += [("weights", m) for m in range(W_UNITS)]
     units += [("text", 2), ("text", 3)]
     units += [("keys", h) for h in range(4)]
-    FIRST_KEYS = len(units) - 4
+    sorted_units = range(4, 12)
 
     with ExitStack() as ctx:
         consts = ctx.enter_context(tc.tile_pool(name="consts", bufs=1))
         codes = ctx.enter_context(tc.tile_pool(name="codes", bufs=1))
+        x_pool = ctx.enter_context(tc.tile_pool(name="x", bufs=5))
         raw_pool = ctx.enter_context(tc.tile_pool(name="raw", bufs=RAW_BUFS))
+        half_pool = ctx.enter_context(tc.tile_pool(name="half", bufs=3))
         grouped_pool = ctx.enter_context(tc.tile_pool(name="grouped", bufs=3))
-        y_pool = ctx.enter_context(tc.tile_pool(name="y", bufs=5))
+        y_pool = ctx.enter_context(tc.tile_pool(name="y", bufs=6))
         q_pool = ctx.enter_context(tc.tile_pool(name="q", bufs=2))
         sq_pool = ctx.enter_context(tc.tile_pool(name="sq", bufs=3))
         norm_pool = ctx.enter_context(tc.tile_pool(name="norm", bufs=2))
-        o_pool = ctx.enter_context(tc.tile_pool(name="o", bufs=6))
+        o_pool = ctx.enter_context(tc.tile_pool(name="o", bufs=5))
         psum = ctx.enter_context(tc.psum_pool(name="psum", bufs=4))
 
         def load_unit(n):
@@ -76,8 +80,14 @@ def tile_crossattention_pb_kernel(tc, text, Wq_w, Wq_b, qn_w, k_norm, out):
         nc.scalar.dma_start(out=vec_rows[4:8, :], in_=qn_w.rearrange("(g c) -> g c", g=4))
 
         raw_of = {}
+
+        def load_next():
+            n = len(raw_of)
+            if n < len(units):
+                raw_of[n] = load_unit(n)
+
         for n in range(RAW_BUFS):
-            raw_of[n] = load_unit(n)
+            load_next()
 
         ident = consts.tile([P, P], F32, name="ident")
         make_identity(nc, ident[:])
@@ -109,18 +119,38 @@ def tile_crossattention_pb_kernel(tc, text, Wq_w, Wq_b, qn_w, k_norm, out):
         for m in range(W_UNITS):
             w_codes.append(codes.tile([P, 2 * PASSES * P], U32, name="w_codes%d" % m, align_bytes=64))
             w_scales.append(codes.tile([P, 2 * PASSES * P], U8, name="w_scales%d" % m, align_bytes=64))
-        text_codes = codes.tile([P, PASSES, TOKENS], U32, name="text_codes", align_bytes=64)
-        text_scales = codes.tile([P, PASSES, TOKENS], U8, name="text_scales", align_bytes=64)
-        key_codes = codes.tile([P, PASSES, TOKENS], U32, name="key_codes", align_bytes=64)
-        key_scales = codes.tile([P, PASSES, TOKENS], U8, name="key_scales", align_bytes=64)
-        q_codes = codes.tile([P, PASSES, TOKENS], U32, name="q_codes", align_bytes=64)
-        q_scales = codes.tile([P, PASSES, TOKENS], U8, name="q_scales", align_bytes=64)
+
+        x_of = {}
+
+        def operand(kind, batch):
+            if (kind, batch) not in x_of:
+                x_codes = x_pool.tile([P, PASSES, BATCH], U32, name="x_codes", align_bytes=64)
+                x_scales = x_pool.tile([P, PASSES, BATCH], U8, name="x_scales", align_bytes=64)
+                x_of[(kind, batch)] = (x_codes, x_scales)
+            return x_of[(kind, batch)]
 
         def transpose_unit(n):
             kind, index = units[n]
-            words = raw_of[n][:].bitcast(F32).rearrange(
+            raw_words = raw_of[n][:].bitcast(F32).rearrange(
                 "p (e g c u) -> p e g c u", e=2, g=PASSES, u=2
             )
+            source = {}
+            for e in range(2):
+                if n in sorted_units:
+                    half = half_pool.tile([P, D], BF16, name="half")
+                    half_words = half[:].bitcast(F32).rearrange(
+                        "p (g u c) -> p g u c", g=PASSES, u=2
+                    )
+                    nc.vector.tensor_copy(
+                        out=half_words, in_=raw_words[:, e].rearrange("p g c u -> p g u c")
+                    )
+                    for g in range(PASSES):
+                        for u in range(2):
+                            source[(e, g, u)] = half_words[:, g, u, :]
+                else:
+                    for g in range(PASSES):
+                        for u in range(2):
+                            source[(e, g, u)] = raw_words[:, e, g, :, u]
             grouped = grouped_pool.tile([P, 2 * D], BF16, name="grouped", align_bytes=64)
             grouped_words = grouped[:].bitcast(F32).rearrange(
                 "p (a x r u) -> p a x r u", a=4, x=2, u=2
@@ -133,7 +163,7 @@ def tile_crossattention_pb_kernel(tc, text, Wq_w, Wq_b, qn_w, k_norm, out):
                     else:
                         e, g = x, a
                     for u in range(2):
-                        nc.tensor.transpose(bank[:, x, u, :], words[:, e, g, :, u], ident[:])
+                        nc.tensor.transpose(bank[:, x, u, :], source[(e, g, u)], ident[:])
                 nc.scalar.copy(
                     out=grouped_words[:, a], in_=bank[:].rearrange("p x u r -> p x r u")
                 )
@@ -146,8 +176,8 @@ def tile_crossattention_pb_kernel(tc, text, Wq_w, Wq_b, qn_w, k_norm, out):
                     out=w_codes[index][:].bitcast(FP8X4), scales=w_scales[index][:], in_=grouped[:]
                 )
                 return
-            dst_codes, dst_scales = (text_codes, text_scales) if kind == "text" else (key_codes, key_scales)
-            cols = slice(index * UNIT_ROWS, (index + 1) * UNIT_ROWS)
+            dst_codes, dst_scales = operand(kind, index // 2)
+            cols = slice((index % 2) * UNIT_ROWS, (index % 2 + 1) * UNIT_ROWS)
             for g in range(PASSES):
                 nc.vector.quantize_mx(
                     out=dst_codes[:, g, cols].bitcast(FP8X4),
@@ -155,41 +185,61 @@ def tile_crossattention_pb_kernel(tc, text, Wq_w, Wq_b, qn_w, k_norm, out):
                     in_=grouped[:, g * 4 * UNIT_ROWS : (g + 1) * 4 * UNIT_ROWS],
                 )
 
+        waiting = []
+
+        def prepare(n):
+            grouped = transpose_unit(n)
+            load_next()
+            for unit, unit_grouped in waiting:
+                quantise_unit(unit, unit_grouped)
+            waiting.clear()
+            if units[n][0] == "weights":
+                waiting.append((n, grouped))
+            else:
+                quantise_unit(n, grouped)
+
         y_of = {}
         acc_of = {}
         inv_of = {}
 
-        def project(block, m):
-            tokens = slice(block * BLOCK, (block + 1) * BLOCK)
+        def project(block, m, gain_engines):
+            first, n = BLOCKS[block]
+            text_codes, text_scales = operand("text", first // BATCH)
+            tokens = slice(first % BATCH, first % BATCH + n)
             for e in range(2):
                 j = 2 * m + e
-                bank = psum.tile([P, BLOCK], F32, name="mm")
-                for g in range(PASSES):
-                    cols = slice((PASSES * e + g) * P, (PASSES * e + g + 1) * P)
+                g, t = divmod(j, 4)
+                bank = psum.tile([P, BATCH], F32, name="mm")
+                for k in range(PASSES):
+                    cols = slice((PASSES * e + k) * P, (PASSES * e + k + 1) * P)
                     nc.tensor.matmul_mx(
-                        out=bank[:],
+                        out=bank[:, 0:n],
                         lhsT=w_codes[m][:, cols].bitcast(FP8X4),
                         lhsT_scale=w_scales[m][:, cols],
-                        rhs=text_codes[:, g, tokens].bitcast(FP8X4),
-                        rhs_scale=text_scales[:, g, tokens],
-                        start=(g == 0),
-                        stop=(g == PASSES - 1),
+                        rhs=text_codes[:, k, tokens].bitcast(FP8X4),
+                        rhs_scale=text_scales[:, k, tokens],
+                        start=(k == 0),
+                        stop=(k == PASSES - 1),
                     )
-                if j % 4 == 0:
-                    y_of[(block, j // 4)] = y_pool.tile([P, 4, BLOCK], F32, name="y4")
-                y4 = y_of[(block, j // 4)]
+                groups = BATCH // n
+                if t == 0 and g % groups == 0:
+                    y_tile = y_pool.tile([P, 4 * BATCH], F32, name="y_tile")
+                    y_views = y_tile[:].rearrange("p (s t c) -> p s t c", s=groups, t=4)
+                    for s in range(groups):
+                        y_of[(block, g + s)] = y_views[:, s]
+                y4 = y_of[(block, g)]
                 if j == 0:
-                    acc_of[block] = norm_pool.tile([P, BLOCK], F32, name="acc")
+                    acc_of[block] = norm_pool.tile([P, BATCH], F32, name="acc")
                     sq = acc_of[block]
                 else:
-                    sq = sq_pool.tile([P, BLOCK], F32, name="sq")
+                    sq = sq_pool.tile([P, BATCH], F32, name="sq")
                 nc.scalar.activation(
-                    out=sq[:], in_=bank[:], func=ACT.Square, bias=bias[:, j : j + 1], scale=1.0
+                    out=sq[:, 0:n], in_=bank[:, 0:n], func=ACT.Square, bias=bias[:, j : j + 1], scale=1.0
                 )
-                if block == 0:
+                if gain_engines[e] == "V":
                     nc.vector.tensor_scalar(
-                        out=y4[:, j % 4, :],
-                        in0=bank[:],
+                        out=y4[:, t, :],
+                        in0=bank[:, 0:n],
                         scalar1=gain[:, j : j + 1],
                         scalar2=gain_bias[:, j : j + 1],
                         op0=ALU.mult,
@@ -197,101 +247,128 @@ def tile_crossattention_pb_kernel(tc, text, Wq_w, Wq_b, qn_w, k_norm, out):
                     )
                 else:
                     nc.scalar.activation(
-                        out=y4[:, j % 4, :],
-                        in_=bank[:],
+                        out=y4[:, t, :],
+                        in_=bank[:, 0:n],
                         func=ACT.Identity,
                         bias=gain_bias[:, j : j + 1],
                         scale=gain[:, j : j + 1],
                     )
                 if j > 0:
                     acc = acc_of[block]
-                    nc.vector.tensor_tensor(out=acc[:], in0=acc[:], in1=sq[:], op=ALU.add)
+                    nc.vector.tensor_tensor(out=acc[:, 0:n], in0=acc[:, 0:n], in1=sq[:, 0:n], op=ALU.add)
 
         def rms_factor(block):
-            bank = psum.tile([P, BLOCK], F32, name="mm")
-            nc.tensor.matmul(out=bank[:], lhsT=mean_w[:], rhs=acc_of[block][:], start=True, stop=True)
-            inv = norm_pool.tile([P, BLOCK], F32, name="inv")
+            n = BLOCKS[block][1]
+            bank = psum.tile([P, BATCH], F32, name="mm")
+            nc.tensor.matmul(
+                out=bank[:, 0:n], lhsT=mean_w[:], rhs=acc_of[block][:, 0:n], start=True, stop=True
+            )
+            inv = norm_pool.tile([P, BATCH], F32, name="inv")
             nc.scalar.activation(
-                out=inv[:], in_=bank[:], func=ACT.Abs_reciprocal_sqrt, bias=eps[:, 0:1], scale=1.0
+                out=inv[:, 0:n], in_=bank[:, 0:n], func=ACT.Abs_reciprocal_sqrt, bias=eps[:, 0:1], scale=1.0
             )
             inv_of[block] = inv
 
+        q_grouped_of = {}
+
         def normalise(block, g):
-            tokens = slice(block * BLOCK, (block + 1) * BLOCK)
-            q_grouped = q_pool.tile([P, 4 * BLOCK], BF16, name="q_grouped", align_bytes=64)
+            n = BLOCKS[block][1]
+            q_grouped = q_pool.tile([P, 4 * BATCH], BF16, name="q_grouped", align_bytes=64)
             nc.vector.tensor_tensor(
-                out=q_grouped[:].rearrange("p (c i t) -> p c t i", i=4, t=4),
-                in0=y_of[(block, g)][:].rearrange("p t (c i) -> p c t i", i=4),
-                in1=inv_of[block][:]
+                out=q_grouped[:, 0 : 4 * n].rearrange("p (c i t) -> p c t i", i=4, t=4),
+                in0=y_of[(block, g)].rearrange("p t (c i) -> p c t i", i=4),
+                in1=inv_of[block][:, 0:n]
                 .rearrange("p (c i) -> p c i", i=4)
                 .unsqueeze(2)
-                .to_broadcast([P, BLOCK // 4, 4, 4]),
+                .to_broadcast([P, n // 4, 4, 4]),
                 op=ALU.mult,
             )
+            q_grouped_of[(block, g)] = q_grouped
+
+        def quantise_q(block, g):
+            first, n = BLOCKS[block]
+            q_codes, q_scales = operand("q", first // BATCH)
+            tokens = slice(first % BATCH, first % BATCH + n)
             nc.vector.quantize_mx(
                 out=q_codes[:, g, tokens].bitcast(FP8X4),
                 scales=q_scales[:, g, tokens],
-                in_=q_grouped[:],
+                in_=q_grouped_of[(block, g)][:, 0 : 4 * n],
             )
 
-        def score_pass(block, g, banks):
-            keys = slice(block * BLOCK, (block + 1) * BLOCK)
-            for i in range(4):
-                tokens = slice(block * BLOCK + i * P, block * BLOCK + (i + 1) * P)
-                nc.tensor.matmul_mx(
-                    out=banks[i][:],
-                    lhsT=q_codes[:, g, tokens].bitcast(FP8X4),
-                    lhsT_scale=q_scales[:, g, tokens],
-                    rhs=key_codes[:, g, keys].bitcast(FP8X4),
-                    rhs_scale=key_scales[:, g, keys],
-                    start=(g == 0),
-                    stop=(g == PASSES - 1),
-                )
-
-        def store_scores(block, banks):
-            for i in range(4):
-                o_sb = o_pool.tile([P, BLOCK], F32, name="o_sb")
-                if block == 1 and i % 2 == 1:
+        def score(block, copy_engines, tag):
+            first, n = BLOCKS[block]
+            q_codes, q_scales = operand("q", first // BATCH)
+            key_codes, key_scales = operand("keys", first // BATCH)
+            banks = [psum.tile([P, BATCH], F32, name="sc%d_%d" % (block, i), tag=tag) for i in range(n // P)]
+            for g in range(PASSES):
+                for i in range(n // P):
+                    tokens = slice(first % BATCH + i * P, first % BATCH + (i + 1) * P)
+                    nc.tensor.matmul_mx(
+                        out=banks[i][:],
+                        lhsT=q_codes[:, g, tokens].bitcast(FP8X4),
+                        lhsT_scale=q_scales[:, g, tokens],
+                        rhs=key_codes[:, g, :].bitcast(FP8X4),
+                        rhs_scale=key_scales[:, g, :],
+                        start=(g == 0),
+                        stop=(g == PASSES - 1),
+                    )
+            for i in range(n // P):
+                o_sb = o_pool.tile([P, BATCH], F32, name="o_sb")
+                if copy_engines[i] == "V":
                     nc.vector.tensor_scalar_mul(out=o_sb[:], in0=banks[i][:], scalar1=SCORE_SCALE)
                 else:
-                    nc.scalar.activation(
-                        out=o_sb[:], in_=banks[i][:], func=ACT.Copy, scale=SCORE_SCALE
-                    )
-                rows = slice(block * BLOCK + i * P, block * BLOCK + (i + 1) * P)
-                nc.sync.dma_start(out=out_rows[rows, :], in_=o_sb[:])
+                    nc.scalar.activation(out=o_sb[:], in_=banks[i][:], func=ACT.Copy, scale=SCORE_SCALE)
+                nc.sync.dma_start(out=out_rows[first + i * P : first + (i + 1) * P, :], in_=o_sb[:])
 
-        grouped_of = {}
-        for n in range(2 * W_UNITS + LEAD):
-            if 1 <= n <= FIRST_KEYS and units[n - 1][0] == "weights":
-                quantise_unit(n - 1, grouped_of[n - 1])
-            if n < FIRST_KEYS:
-                grouped_of[n] = transpose_unit(n)
-                raw_of[n + RAW_BUFS] = load_unit(n + RAW_BUFS)
-                if units[n][0] == "text":
-                    quantise_unit(n, grouped_of[n])
+        next_unit = 0
+        for n in range(LEAD + 1):
+            prepare(n)
             if n == 1:
                 spread_bias_and_gain()
-            if n >= LEAD:
-                block, m = divmod(n - LEAD, W_UNITS)
-                project(block, m)
-                if block == 1 and m == 0:
-                    rms_factor(0)
-                if block == 1 and m % 2 == 0:
-                    normalise(0, m // 2)
+        next_unit = LEAD + 1
+        for m in range(W_UNITS):
+            if next_unit < 12:
+                prepare(next_unit)
+                next_unit += 1
+            project(0, m, "VS")
 
-        grouped_of[FIRST_KEYS] = transpose_unit(FIRST_KEYS)
-        rms_factor(1)
+        for m in range(W_UNITS):
+            if next_unit < 12:
+                prepare(next_unit)
+                next_unit += 1
+            project(1, m, "SS")
+            if m == 0:
+                rms_factor(0)
+            if m in (2, 6):
+                prepare(next_unit)
+                next_unit += 1
+            if m % 2 == 1:
+                normalise(0, m // 2)
+            elif m > 0:
+                quantise_q(0, m // 2 - 1)
+
+        for m in range(W_UNITS):
+            project(2, m, "SS")
+            if m == 0:
+                quantise_q(0, 3)
+                rms_factor(1)
+            if m in (2,):
+                prepare(next_unit)
+                next_unit += 1
+            if m % 2 == 1:
+                normalise(1, m // 2)
+            elif m > 0:
+                quantise_q(1, m // 2 - 1)
+            if m == 7:
+                score(0, "SSSS", "tp")
+
+        quantise_q(1, 3)
+        rms_factor(2)
+        while next_unit < len(units):
+            prepare(next_unit)
+            next_unit += 1
+        score(1, "SS", "mm")
         for g in range(PASSES):
-            if g + 1 < 4:
-                grouped_of[FIRST_KEYS + g + 1] = transpose_unit(FIRST_KEYS + g + 1)
-            quantise_unit(FIRST_KEYS + g, grouped_of[FIRST_KEYS + g])
-            if g == 2:
-                banks0 = [psum.tile([P, BLOCK], F32, name="sc%d" % i, tag="mm") for i in range(4)]
-                for gg in range(PASSES):
-                    score_pass(0, gg, banks0)
-                store_scores(0, banks0)
-            normalise(1, g)
-        banks1 = [psum.tile([P, BLOCK], F32, name="sd%d" % i, tag="tp") for i in range(4)]
-        for g in range(PASSES):
-            score_pass(1, g, banks1)
-        store_scores(1, banks1)
+            normalise(2, g)
+            quantise_q(2, g)
+        score(2, "SV", "mm")

@@ -40,7 +40,8 @@ def tile_crossattention_pb_kernel(tc, text, Wq_w, Wq_b, qn_w, k_norm, out):
     units += [("weights", m) for m in range(W_UNITS)]
     units += [("text", 2), ("text", 3)]
     units += [("keys", h) for h in range(4)]
-    sorted_units = range(4, 12)
+    shared_units = range(3)
+    sorted_units = ()
 
     with ExitStack() as ctx:
         consts = ctx.enter_context(tc.tile_pool(name="consts", bufs=1))
@@ -164,9 +165,14 @@ def tile_crossattention_pb_kernel(tc, text, Wq_w, Wq_b, qn_w, k_norm, out):
                         e, g = x, a
                     for u in range(2):
                         nc.tensor.transpose(bank[:, x, u, :], source[(e, g, u)], ident[:])
-                nc.scalar.copy(
-                    out=grouped_words[:, a], in_=bank[:].rearrange("p x u r -> p x r u")
-                )
+                if n in shared_units and a % 2 == 1:
+                    nc.vector.tensor_copy(
+                        out=grouped_words[:, a], in_=bank[:].rearrange("p x u r -> p x r u")
+                    )
+                else:
+                    nc.scalar.copy(
+                        out=grouped_words[:, a], in_=bank[:].rearrange("p x u r -> p x r u")
+                    )
             return grouped
 
         def quantise_unit(n, grouped):
@@ -206,14 +212,24 @@ def tile_crossattention_pb_kernel(tc, text, Wq_w, Wq_b, qn_w, k_norm, out):
             first, n = BLOCKS[block]
             text_codes, text_scales = operand("text", first // BATCH)
             tokens = slice(first % BATCH, first % BATCH + n)
+            wide = n == BATCH
+            banks = []
+            squares = []
             for e in range(2):
-                j = 2 * m + e
-                g, t = divmod(j, 4)
-                bank = psum.tile([P, BATCH], F32, name="mm")
+                if wide or e == 0:
+                    bank = psum.tile([P, BATCH], F32, name="mm")
+                    if m == 0 and e == 0:
+                        acc_of[block] = norm_pool.tile([P, BATCH], F32, name="acc")
+                        sq = acc_of[block]
+                    else:
+                        sq = sq_pool.tile([P, BATCH], F32, name="sq")
+                half = slice(0, n) if wide else slice(e * n, (e + 1) * n)
+                banks.append(bank[:, half])
+                squares.append(sq[:, half])
                 for k in range(PASSES):
                     cols = slice((PASSES * e + k) * P, (PASSES * e + k + 1) * P)
                     nc.tensor.matmul_mx(
-                        out=bank[:, 0:n],
+                        out=banks[e],
                         lhsT=w_codes[m][:, cols].bitcast(FP8X4),
                         lhsT_scale=w_scales[m][:, cols],
                         rhs=text_codes[:, k, tokens].bitcast(FP8X4),
@@ -221,6 +237,9 @@ def tile_crossattention_pb_kernel(tc, text, Wq_w, Wq_b, qn_w, k_norm, out):
                         start=(k == 0),
                         stop=(k == PASSES - 1),
                     )
+            for e in range(2):
+                j = 2 * m + e
+                g, t = divmod(j, 4)
                 groups = BATCH // n
                 if t == 0 and g % groups == 0:
                     y_tile = y_pool.tile([P, 4 * BATCH], F32, name="y_tile")
@@ -228,18 +247,13 @@ def tile_crossattention_pb_kernel(tc, text, Wq_w, Wq_b, qn_w, k_norm, out):
                     for s in range(groups):
                         y_of[(block, g + s)] = y_views[:, s]
                 y4 = y_of[(block, g)]
-                if j == 0:
-                    acc_of[block] = norm_pool.tile([P, BATCH], F32, name="acc")
-                    sq = acc_of[block]
-                else:
-                    sq = sq_pool.tile([P, BATCH], F32, name="sq")
                 nc.scalar.activation(
-                    out=sq[:, 0:n], in_=bank[:, 0:n], func=ACT.Square, bias=bias[:, j : j + 1], scale=1.0
+                    out=squares[e], in_=banks[e], func=ACT.Square, bias=bias[:, j : j + 1], scale=1.0
                 )
                 if gain_engines[e] == "V":
                     nc.vector.tensor_scalar(
                         out=y4[:, t, :],
-                        in0=bank[:, 0:n],
+                        in0=banks[e],
                         scalar1=gain[:, j : j + 1],
                         scalar2=gain_bias[:, j : j + 1],
                         op0=ALU.mult,
@@ -248,21 +262,26 @@ def tile_crossattention_pb_kernel(tc, text, Wq_w, Wq_b, qn_w, k_norm, out):
                 else:
                     nc.scalar.activation(
                         out=y4[:, t, :],
-                        in_=bank[:, 0:n],
+                        in_=banks[e],
                         func=ACT.Identity,
                         bias=gain_bias[:, j : j + 1],
                         scale=gain[:, j : j + 1],
                     )
-                if j > 0:
+                if j > 0 and (wide or (e == 1 and m > 0)):
                     acc = acc_of[block]
-                    nc.vector.tensor_tensor(out=acc[:, 0:n], in0=acc[:, 0:n], in1=sq[:, 0:n], op=ALU.add)
+                    nc.vector.tensor_tensor(out=acc[:], in0=acc[:], in1=sq[:] if not wide else squares[e], op=ALU.add)
 
         def rms_factor(block):
             n = BLOCKS[block][1]
             bank = psum.tile([P, BATCH], F32, name="mm")
-            nc.tensor.matmul(
-                out=bank[:, 0:n], lhsT=mean_w[:], rhs=acc_of[block][:, 0:n], start=True, stop=True
-            )
+            for h in range(BATCH // n):
+                nc.tensor.matmul(
+                    out=bank[:, 0:n],
+                    lhsT=mean_w[:],
+                    rhs=acc_of[block][:, h * n : (h + 1) * n],
+                    start=(h == 0),
+                    stop=(h == BATCH // n - 1),
+                )
             inv = norm_pool.tile([P, BATCH], F32, name="inv")
             nc.scalar.activation(
                 out=inv[:, 0:n], in_=bank[:, 0:n], func=ACT.Abs_reciprocal_sqrt, bias=eps[:, 0:1], scale=1.0
@@ -330,7 +349,7 @@ def tile_crossattention_pb_kernel(tc, text, Wq_w, Wq_b, qn_w, k_norm, out):
             if next_unit < 12:
                 prepare(next_unit)
                 next_unit += 1
-            project(0, m, "VS")
+            project(0, m, "VV")
 
         for m in range(W_UNITS):
             if next_unit < 12:

@@ -40,8 +40,8 @@ def tile_crossattention_pb_kernel(tc, text, Wq_w, Wq_b, qn_w, k_norm, out):
     units += [("weights", m) for m in range(W_UNITS)]
     units += [("text", 2), ("text", 3)]
     units += [("keys", h) for h in range(4)]
-    shared_units = range(3)
-    sorted_units = ()
+    shared_units = range(2)
+    sorted_units = range(5, 12)
 
     with ExitStack() as ctx:
         consts = ctx.enter_context(tc.tile_pool(name="consts", bufs=1))
@@ -349,7 +349,7 @@ def tile_crossattention_pb_kernel(tc, text, Wq_w, Wq_b, qn_w, k_norm, out):
             if next_unit < 12:
                 prepare(next_unit)
                 next_unit += 1
-            project(0, m, "VV")
+            project(0, m, "VS")
 
         for m in range(W_UNITS):
             if next_unit < 12:

@@ -26,7 +26,7 @@ FLOPS = 2 * TOKENS * D * D + 2 * TOKENS * BATCH * D
 BLOCKS = ((0, 512), (512, 256), (768, 256))
 
 RAW_BUFS = 3
-FIRST_PIECES = 4
+PIECES = {0: 2, 1: 1, 2: 1}
 LEAD = 4
 
 
@@ -46,13 +46,14 @@ def tile_crossattention_pb_kernel(tc, text, Wq_w, Wq_b, qn_w, k_norm, out):
     with ExitStack() as ctx:
         consts = ctx.enter_context(tc.tile_pool(name="consts", bufs=1))
         codes = ctx.enter_context(tc.tile_pool(name="codes", bufs=1))
-        x_pool = ctx.enter_context(tc.tile_pool(name="x", bufs=5))
+        x_pool = ctx.enter_context(tc.tile_pool(name="x", bufs=2))
+        unit_pool = ctx.enter_context(tc.tile_pool(name="unit", bufs=6))
         raw_pool = ctx.enter_context(tc.tile_pool(name="raw", bufs=RAW_BUFS))
         half_pool = ctx.enter_context(tc.tile_pool(name="half", bufs=3))
         grouped_pool = ctx.enter_context(tc.tile_pool(name="grouped", bufs=3))
         y_pool = ctx.enter_context(tc.tile_pool(name="y", bufs=6))
         q_pool = ctx.enter_context(tc.tile_pool(name="q", bufs=2))
-        sq_pool = ctx.enter_context(tc.tile_pool(name="sq", bufs=3))
+        sq_pool = ctx.enter_context(tc.tile_pool(name="sq", bufs=4))
         norm_pool = ctx.enter_context(tc.tile_pool(name="norm", bufs=2))
         o_pool = ctx.enter_context(tc.tile_pool(name="o", bufs=5))
         psum = ctx.enter_context(tc.psum_pool(name="psum", bufs=4))
@@ -69,10 +70,13 @@ def tile_crossattention_pb_kernel(tc, text, Wq_w, Wq_b, qn_w, k_norm, out):
             else:
                 view = key_rows[rows, :].rearrange("(e p) k -> p e k", e=2)
             raw_rows = raw[:].rearrange("p (e k) -> p e k", e=2)
-            pieces = FIRST_PIECES if n == 0 else 1
-            for c in range(pieces):
-                cols = slice(c * D // pieces, (c + 1) * D // pieces)
-                nc.sync.dma_start(out=raw_rows[:, :, cols], in_=view[:, :, cols])
+            if n in PIECES:
+                for e in range(2):
+                    for c in range(PIECES[n]):
+                        cols = slice(c * D // PIECES[n], (c + 1) * D // PIECES[n])
+                        nc.sync.dma_start(out=raw_rows[:, e, cols], in_=view[:, e, cols])
+            else:
+                nc.sync.dma_start(out=raw_rows, in_=view)
             return raw
 
         vec_rows = consts.tile([P, 4 * P], BF16, name="vec_rows")
@@ -122,6 +126,7 @@ def tile_crossattention_pb_kernel(tc, text, Wq_w, Wq_b, qn_w, k_norm, out):
             w_scales.append(codes.tile([P, 2 * PASSES * P], U8, name="w_scales%d" % m, align_bytes=64))
 
         x_of = {}
+        unit_operand_of = {}
 
         def operand(kind, batch):
             if (kind, batch) not in x_of:
@@ -153,25 +158,28 @@ def tile_crossattention_pb_kernel(tc, text, Wq_w, Wq_b, qn_w, k_norm, out):
                         for u in range(2):
                             source[(e, g, u)] = raw_words[:, e, g, :, u]
             grouped = grouped_pool.tile([P, 2 * D], BF16, name="grouped", align_bytes=64)
-            grouped_words = grouped[:].bitcast(F32).rearrange(
-                "p (a x r u) -> p a x r u", a=4, x=2, u=2
-            )
+            if kind == "weights":
+                grouped_words = grouped[:].bitcast(F32).rearrange(
+                    "p (e h x r u) -> p e h x r u", e=2, h=2, x=2, u=2
+                )
+            else:
+                grouped_words = grouped[:].bitcast(F32).rearrange(
+                    "p (h x e r u) -> p e h x r u", e=2, h=2, x=2, u=2
+                )
             for a in range(4):
+                e, h = divmod(a, 2)
                 bank = psum.tile([P, 2, 2, P], F32, name="tp")
                 for x in range(2):
-                    if kind == "weights":
-                        e, g = a // 2, 2 * (a % 2) + x
-                    else:
-                        e, g = x, a
+                    g = 2 * h + x
                     for u in range(2):
                         nc.tensor.transpose(bank[:, x, u, :], source[(e, g, u)], ident[:])
                 if n in shared_units and a % 2 == 1:
                     nc.vector.tensor_copy(
-                        out=grouped_words[:, a], in_=bank[:].rearrange("p x u r -> p x r u")
+                        out=grouped_words[:, e, h], in_=bank[:].rearrange("p x u r -> p x r u")
                     )
                 else:
                     nc.scalar.copy(
-                        out=grouped_words[:, a], in_=bank[:].rearrange("p x u r -> p x r u")
+                        out=grouped_words[:, e, h], in_=bank[:].rearrange("p x u r -> p x r u")
                     )
             return grouped
 
@@ -182,8 +190,16 @@ def tile_crossattention_pb_kernel(tc, text, Wq_w, Wq_b, qn_w, k_norm, out):
                     out=w_codes[index][:].bitcast(FP8X4), scales=w_scales[index][:], in_=grouped[:]
                 )
                 return
-            dst_codes, dst_scales = operand(kind, index // 2)
-            cols = slice((index % 2) * UNIT_ROWS, (index % 2 + 1) * UNIT_ROWS)
+            if kind == "keys" or index >= 2:
+                unit_codes = unit_pool.tile([P, PASSES * UNIT_ROWS], U32, name="unit_codes", align_bytes=64)
+                unit_scales = unit_pool.tile([P, PASSES * UNIT_ROWS], U8, name="unit_scales", align_bytes=64)
+                nc.vector.quantize_mx(
+                    out=unit_codes[:].bitcast(FP8X4), scales=unit_scales[:], in_=grouped[:]
+                )
+                unit_operand_of[(kind, index)] = (unit_codes, unit_scales)
+                return
+            dst_codes, dst_scales = operand(kind, 0)
+            cols = slice(index * UNIT_ROWS, (index + 1) * UNIT_ROWS)
             for g in range(PASSES):
                 nc.vector.quantize_mx(
                     out=dst_codes[:, g, cols].bitcast(FP8X4),
@@ -210,8 +226,15 @@ def tile_crossattention_pb_kernel(tc, text, Wq_w, Wq_b, qn_w, k_norm, out):
 
         def project(block, m, gain_engines):
             first, n = BLOCKS[block]
-            text_codes, text_scales = operand("text", first // BATCH)
-            tokens = slice(first % BATCH, first % BATCH + n)
+            if block == 0:
+                text_codes, text_scales = operand("text", 0)
+                text_views = [(text_codes[:, k, :], text_scales[:, k, :]) for k in range(PASSES)]
+            else:
+                text_codes, text_scales = unit_operand_of[("text", first // UNIT_ROWS)]
+                text_views = []
+                for k in range(PASSES):
+                    rows = slice(k * UNIT_ROWS, (k + 1) * UNIT_ROWS)
+                    text_views.append((text_codes[:, rows], text_scales[:, rows]))
             wide = n == BATCH
             banks = []
             squares = []
@@ -232,8 +255,8 @@ def tile_crossattention_pb_kernel(tc, text, Wq_w, Wq_b, qn_w, k_norm, out):
                         out=banks[e],
                         lhsT=w_codes[m][:, cols].bitcast(FP8X4),
                         lhsT_scale=w_scales[m][:, cols],
-                        rhs=text_codes[:, k, tokens].bitcast(FP8X4),
-                        rhs_scale=text_scales[:, k, tokens],
+                        rhs=text_views[k][0].bitcast(FP8X4),
+                        rhs_scale=text_views[k][1],
                         start=(k == 0),
                         stop=(k == PASSES - 1),
                     )
@@ -314,30 +337,65 @@ def tile_crossattention_pb_kernel(tc, text, Wq_w, Wq_b, qn_w, k_norm, out):
                 in_=q_grouped_of[(block, g)][:, 0 : 4 * n],
             )
 
-        def score(block, copy_engines, tag):
+        score_of = {}
+
+        def score(block, parts, tag):
             first, n = BLOCKS[block]
-            q_codes, q_scales = operand("q", first // BATCH)
-            key_codes, key_scales = operand("keys", first // BATCH)
-            banks = [psum.tile([P, BATCH], F32, name="sc%d_%d" % (block, i), tag=tag) for i in range(n // P)]
-            for g in range(PASSES):
-                for i in range(n // P):
-                    tokens = slice(first % BATCH + i * P, first % BATCH + (i + 1) * P)
-                    nc.tensor.matmul_mx(
-                        out=banks[i][:],
-                        lhsT=q_codes[:, g, tokens].bitcast(FP8X4),
-                        lhsT_scale=q_scales[:, g, tokens],
-                        rhs=key_codes[:, g, :].bitcast(FP8X4),
-                        rhs_scale=key_scales[:, g, :],
-                        start=(g == 0),
-                        stop=(g == PASSES - 1),
-                    )
-            for i in range(n // P):
+            batch = first // BATCH
+            q_codes, q_scales = operand("q", batch)
+
+            def multiply_keys(out, i, h, g):
+                key_codes, key_scales = unit_operand_of[("keys", 2 * batch + h)]
+                tokens = slice(first % BATCH + i * P, first % BATCH + (i + 1) * P)
+                rows = slice(g * UNIT_ROWS, (g + 1) * UNIT_ROWS)
+                nc.tensor.matmul_mx(
+                    out=out,
+                    lhsT=q_codes[:, g, tokens].bitcast(FP8X4),
+                    lhsT_scale=q_scales[:, g, tokens],
+                    rhs=key_codes[:, rows].bitcast(FP8X4),
+                    rhs_scale=key_scales[:, rows],
+                    start=(g == 0),
+                    stop=(g == PASSES - 1),
+                )
+
+            banks = []
+            for p in range(len(parts)):
+                bank = psum.tile([P, BATCH], F32, name="sc%d_%d" % (block, len(score_of) + p), tag=tag)
+                banks.append(bank)
+            if len(parts[0]) == 2:
+                for bank, part in zip(banks, parts):
+                    for x in range(2):
+                        for g in range(PASSES):
+                            i, h = part[x]
+                            multiply_keys(bank[:, x * UNIT_ROWS : (x + 1) * UNIT_ROWS], i, h, g)
+            else:
+                for g in range(PASSES):
+                    for bank, part in zip(banks, parts):
+                        i, h = part[0]
+                        multiply_keys(bank[:, 0:UNIT_ROWS], i, h, g)
+            for bank, part in zip(banks, parts):
+                score_of[(block, part)] = bank
+
+        def store_scores(block, parts, copy_engines):
+            first, n = BLOCKS[block]
+            for part, engine in zip(parts, copy_engines):
+                bank = score_of[(block, part)]
+                width = len(part) * UNIT_ROWS
+                i, h = part[0]
                 o_sb = o_pool.tile([P, BATCH], F32, name="o_sb")
-                if copy_engines[i] == "V":
-                    nc.vector.tensor_scalar_mul(out=o_sb[:], in0=banks[i][:], scalar1=SCORE_SCALE)
+                if engine == "V":
+                    nc.vector.tensor_scalar_mul(out=o_sb[:, 0:width], in0=bank[:, 0:width], scalar1=SCORE_SCALE)
                 else:
-                    nc.scalar.activation(out=o_sb[:], in_=banks[i][:], func=ACT.Copy, scale=SCORE_SCALE)
-                nc.sync.dma_start(out=out_rows[first + i * P : first + (i + 1) * P, :], in_=o_sb[:])
+                    nc.scalar.activation(
+                        out=o_sb[:, 0:width], in_=bank[:, 0:width], func=ACT.Copy, scale=SCORE_SCALE
+                    )
+                rows = slice(first + i * P, first + (i + 1) * P)
+                nc.sync.dma_start(
+                    out=out_rows[rows, h * UNIT_ROWS : h * UNIT_ROWS + width], in_=o_sb[:, 0:width]
+                )
+
+        whole = [((i, 0), (i, 1)) for i in range(4)]
+        single = [((i, h),) for i in range(2) for h in range(2)]
 
         next_unit = 0
         for n in range(LEAD + 1):
@@ -351,14 +409,13 @@ def tile_crossattention_pb_kernel(tc, text, Wq_w, Wq_b, qn_w, k_norm, out):
                 next_unit += 1
             project(0, m, "VS")
 
+        prepare(next_unit)
+        next_unit += 1
         for m in range(W_UNITS):
-            if next_unit < 12:
-                prepare(next_unit)
-                next_unit += 1
             project(1, m, "SS")
             if m == 0:
                 rms_factor(0)
-            if m in (2, 6):
+            if m == 4:
                 prepare(next_unit)
                 next_unit += 1
             if m % 2 == 1:
@@ -366,28 +423,33 @@ def tile_crossattention_pb_kernel(tc, text, Wq_w, Wq_b, qn_w, k_norm, out):
             elif m > 0:
                 quantise_q(0, m // 2 - 1)
 
-        for m in range(W_UNITS):
+        for m in range(W_UNITS - 1):
             project(2, m, "SS")
             if m == 0:
                 quantise_q(0, 3)
                 rms_factor(1)
-            if m in (2,):
+            if m in (2, 5):
                 prepare(next_unit)
                 next_unit += 1
             if m % 2 == 1:
                 normalise(1, m // 2)
             elif m > 0:
                 quantise_q(1, m // 2 - 1)
-            if m == 7:
-                score(0, "SSSS", "tp")
 
-        quantise_q(1, 3)
+        ctx.enter_context(tc.manual_schedule())
+        project(2, W_UNITS - 1, "SS")
+        score(0, whole[0:2], "tp")
         rms_factor(2)
-        while next_unit < len(units):
-            prepare(next_unit)
-            next_unit += 1
-        score(1, "SS", "mm")
+        normalise(1, 3)
+        quantise_q(1, 3)
+        score(0, whole[2:4], "tp")
+        store_scores(0, whole, "SSSS")
+        score(1, whole[0:2], "mm")
+        store_scores(1, whole[0:2], "SS")
         for g in range(PASSES):
             normalise(2, g)
-            quantise_q(2, g)
-        score(2, "SV", "mm")
+            if g > 0:
+                quantise_q(2, g - 1)
+        quantise_q(2, 3)
+        score(2, single, "mm")
+        store_scores(2, single, "SVSV")

from contextlib import ExitStack

import concourse.mybir as mybir
from concourse.masks import make_identity

F32 = mybir.dt.float32
BF16 = mybir.dt.bfloat16
U32 = mybir.dt.uint32
U8 = mybir.dt.uint8
FP8X4 = mybir.dt.float8_e4m3fn_x4
ACT = mybir.ActivationFunctionType
ALU = mybir.AluOpType

P = 128
D = 2048
PASSES = 4
TOKENS = 1024
BATCH = 512
UNIT_ROWS = 256
W_UNITS = D // UNIT_ROWS
EPS = 1e-6
SCORE_SCALE = 1.0 / (2048.0 ** 0.5)

FLOPS = 2 * TOKENS * D * D + 2 * TOKENS * BATCH * D

BLOCKS = ((0, 512), (512, 256), (768, 256))

RAW_BUFS = 3
PIECES = {0: 2, 1: 1, 2: 1}
LEAD = 4


def tile_crossattention_pb_kernel(tc, text, Wq_w, Wq_b, qn_w, k_norm, out):
    nc = tc.nc
    text_rows = text.flatten_outer_dims()
    key_rows = k_norm.flatten_outer_dims()
    out_rows = out.flatten_outer_dims()

    units = [("text", 0), ("text", 1)]
    units += [("weights", m) for m in range(W_UNITS)]
    units += [("text", 2), ("text", 3)]
    units += [("keys", h) for h in range(4)]
    shared_units = range(2)
    sorted_units = range(5, 12)

    with ExitStack() as ctx:
        consts = ctx.enter_context(tc.tile_pool(name="consts", bufs=1))
        codes = ctx.enter_context(tc.tile_pool(name="codes", bufs=1))
        x_pool = ctx.enter_context(tc.tile_pool(name="x", bufs=2))
        unit_pool = ctx.enter_context(tc.tile_pool(name="unit", bufs=6))
        raw_pool = ctx.enter_context(tc.tile_pool(name="raw", bufs=RAW_BUFS))
        half_pool = ctx.enter_context(tc.tile_pool(name="half", bufs=3))
        grouped_pool = ctx.enter_context(tc.tile_pool(name="grouped", bufs=3))
        y_pool = ctx.enter_context(tc.tile_pool(name="y", bufs=6))
        q_pool = ctx.enter_context(tc.tile_pool(name="q", bufs=2))
        sq_pool = ctx.enter_context(tc.tile_pool(name="sq", bufs=4))
        norm_pool = ctx.enter_context(tc.tile_pool(name="norm", bufs=2))
        o_pool = ctx.enter_context(tc.tile_pool(name="o", bufs=5))
        psum = ctx.enter_context(tc.psum_pool(name="psum", bufs=4))

        def load_unit(n):
            kind, index = units[n]
            rows = slice(index * UNIT_ROWS, (index + 1) * UNIT_ROWS)
            raw = raw_pool.tile([P, 2 * D], BF16, name="raw")
            if kind == "weights":
                group = slice((index // 2) * 512, (index // 2 + 1) * 512)
                view = Wq_w[group, :].rearrange("(p h e) k -> p h e k", h=2, e=2)[:, index % 2]
            elif kind == "text":
                view = text_rows[rows, :].rearrange("(e p) k -> p e k", e=2)
            else:
                view = key_rows[rows, :].rearrange("(e p) k -> p e k", e=2)
            raw_rows = raw[:].rearrange("p (e k) -> p e k", e=2)
            if n in PIECES:
                for e in range(2):
                    for c in range(PIECES[n]):
                        cols = slice(c * D // PIECES[n], (c + 1) * D // PIECES[n])
                        nc.sync.dma_start(out=raw_rows[:, e, cols], in_=view[:, e, cols])
            else:
                nc.sync.dma_start(out=raw_rows, in_=view)
            return raw

        vec_rows = consts.tile([P, 4 * P], BF16, name="vec_rows")
        nc.vector.memset(vec_rows[:], 0.0)
        nc.scalar.dma_start(out=vec_rows[0:4, :], in_=Wq_b.rearrange("(g c) -> g c", g=4))
        nc.scalar.dma_start(out=vec_rows[4:8, :], in_=qn_w.rearrange("(g c) -> g c", g=4))

        raw_of = {}

        def load_next():
            n = len(raw_of)
            if n < len(units):
                raw_of[n] = load_unit(n)

        for n in range(RAW_BUFS):
            load_next()

        ident = consts.tile([P, P], F32, name="ident")
        make_identity(nc, ident[:])
        mean_w = consts.tile([P, P], F32, name="mean_w")
        nc.vector.memset(mean_w[:], 1.0 / D)
        eps = consts.tile([P, 1], F32, name="eps")
        nc.vector.memset(eps[:], EPS)
        warm = consts.tile([P, 1], F32, name="warm")
        nc.scalar.activation(out=warm[:], in_=eps[:], func=ACT.Abs_reciprocal_sqrt)

        bias_gain = consts.tile([P, 32], F32, name="bias_gain")
        bias = bias_gain[:, 0:16]
        gain = bias_gain[:, 16:32]
        gain_bias = consts.tile([P, 16], F32, name="gain_bias")

        def spread_bias_and_gain():
            vec_bank = psum.tile([P, 2, 2, P], F32, name="tp")
            vec_words = vec_rows[:].bitcast(F32).rearrange("p (c u) -> p c u", u=2)
            for u in range(2):
                nc.tensor.transpose(vec_bank[:, 0, u, :], vec_words[:, :, u], ident[:])
            nc.vector.tensor_copy(
                out=bias_gain[:].rearrange("p (r u v) -> p r u v", u=2, v=2),
                in_=vec_bank[:, 0, :, 0:8].bitcast(BF16).rearrange("p u (r v) -> p r u v", v=2),
            )
            nc.vector.tensor_tensor(out=gain_bias[:], in0=gain, in1=bias, op=ALU.mult)

        w_codes = []
        w_scales = []
        for m in range(W_UNITS):
            w_codes.append(codes.tile([P, 2 * PASSES * P], U32, name="w_codes%d" % m, align_bytes=64))
            w_scales.append(codes.tile([P, 2 * PASSES * P], U8, name="w_scales%d" % m, align_bytes=64))

        x_of = {}
        unit_operand_of = {}

        def operand(kind, batch):
            if (kind, batch) not in x_of:
                x_codes = x_pool.tile([P, PASSES, BATCH], U32, name="x_codes", align_bytes=64)
                x_scales = x_pool.tile([P, PASSES, BATCH], U8, name="x_scales", align_bytes=64)
                x_of[(kind, batch)] = (x_codes, x_scales)
            return x_of[(kind, batch)]

        def transpose_unit(n):
            kind, index = units[n]
            raw_words = raw_of[n][:].bitcast(F32).rearrange(
                "p (e g c u) -> p e g c u", e=2, g=PASSES, u=2
            )
            source = {}
            for e in range(2):
                if n in sorted_units:
                    half = half_pool.tile([P, D], BF16, name="half")
                    half_words = half[:].bitcast(F32).rearrange(
                        "p (g u c) -> p g u c", g=PASSES, u=2
                    )
                    nc.vector.tensor_copy(
                        out=half_words, in_=raw_words[:, e].rearrange("p g c u -> p g u c")
                    )
                    for g in range(PASSES):
                        for u in range(2):
                            source[(e, g, u)] = half_words[:, g, u, :]
                else:
                    for g in range(PASSES):
                        for u in range(2):
                            source[(e, g, u)] = raw_words[:, e, g, :, u]
            grouped = grouped_pool.tile([P, 2 * D], BF16, name="grouped", align_bytes=64)
            if kind == "weights":
                grouped_words = grouped[:].bitcast(F32).rearrange(
                    "p (e h x r u) -> p e h x r u", e=2, h=2, x=2, u=2
                )
            else:
                grouped_words = grouped[:].bitcast(F32).rearrange(
                    "p (h x e r u) -> p e h x r u", e=2, h=2, x=2, u=2
                )
            for a in range(4):
                e, h = divmod(a, 2)
                bank = psum.tile([P, 2, 2, P], F32, name="tp")
                for x in range(2):
                    g = 2 * h + x
                    for u in range(2):
                        nc.tensor.transpose(bank[:, x, u, :], source[(e, g, u)], ident[:])
                if n in shared_units and a % 2 == 1:
                    nc.vector.tensor_copy(
                        out=grouped_words[:, e, h], in_=bank[:].rearrange("p x u r -> p x r u")
                    )
                else:
                    nc.scalar.copy(
                        out=grouped_words[:, e, h], in_=bank[:].rearrange("p x u r -> p x r u")
                    )
            return grouped

        def quantise_unit(n, grouped):
            kind, index = units[n]
            if kind == "weights":
                nc.vector.quantize_mx(
                    out=w_codes[index][:].bitcast(FP8X4), scales=w_scales[index][:], in_=grouped[:]
                )
                return
            if kind == "keys" or index >= 2:
                unit_codes = unit_pool.tile([P, PASSES * UNIT_ROWS], U32, name="unit_codes", align_bytes=64)
                unit_scales = unit_pool.tile([P, PASSES * UNIT_ROWS], U8, name="unit_scales", align_bytes=64)
                nc.vector.quantize_mx(
                    out=unit_codes[:].bitcast(FP8X4), scales=unit_scales[:], in_=grouped[:]
                )
                unit_operand_of[(kind, index)] = (unit_codes, unit_scales)
                return
            dst_codes, dst_scales = operand(kind, 0)
            cols = slice(index * UNIT_ROWS, (index + 1) * UNIT_ROWS)
            for g in range(PASSES):
                nc.vector.quantize_mx(
                    out=dst_codes[:, g, cols].bitcast(FP8X4),
                    scales=dst_scales[:, g, cols],
                    in_=grouped[:, g * 4 * UNIT_ROWS : (g + 1) * 4 * UNIT_ROWS],
                )

        waiting = []

        def prepare(n):
            grouped = transpose_unit(n)
            load_next()
            for unit, unit_grouped in waiting:
                quantise_unit(unit, unit_grouped)
            waiting.clear()
            if units[n][0] == "weights":
                waiting.append((n, grouped))
            else:
                quantise_unit(n, grouped)

        y_of = {}
        acc_of = {}
        inv_of = {}

        def project(block, m, gain_engines):
            first, n = BLOCKS[block]
            if block == 0:
                text_codes, text_scales = operand("text", 0)
                text_views = [(text_codes[:, k, :], text_scales[:, k, :]) for k in range(PASSES)]
            else:
                text_codes, text_scales = unit_operand_of[("text", first // UNIT_ROWS)]
                text_views = []
                for k in range(PASSES):
                    rows = slice(k * UNIT_ROWS, (k + 1) * UNIT_ROWS)
                    text_views.append((text_codes[:, rows], text_scales[:, rows]))
            wide = n == BATCH
            banks = []
            squares = []
            for e in range(2):
                if wide or e == 0:
                    bank = psum.tile([P, BATCH], F32, name="mm")
                    if m == 0 and e == 0:
                        acc_of[block] = norm_pool.tile([P, BATCH], F32, name="acc")
                        sq = acc_of[block]
                    else:
                        sq = sq_pool.tile([P, BATCH], F32, name="sq")
                half = slice(0, n) if wide else slice(e * n, (e + 1) * n)
                banks.append(bank[:, half])
                squares.append(sq[:, half])
                for k in range(PASSES):
                    cols = slice((PASSES * e + k) * P, (PASSES * e + k + 1) * P)
                    nc.tensor.matmul_mx(
                        out=banks[e],
                        lhsT=w_codes[m][:, cols].bitcast(FP8X4),
                        lhsT_scale=w_scales[m][:, cols],
                        rhs=text_views[k][0].bitcast(FP8X4),
                        rhs_scale=text_views[k][1],
                        start=(k == 0),
                        stop=(k == PASSES - 1),
                    )
            for e in range(2):
                j = 2 * m + e
                g, t = divmod(j, 4)
                groups = BATCH // n
                if t == 0 and g % groups == 0:
                    y_tile = y_pool.tile([P, 4 * BATCH], F32, name="y_tile")
                    y_views = y_tile[:].rearrange("p (s t c) -> p s t c", s=groups, t=4)
                    for s in range(groups):
                        y_of[(block, g + s)] = y_views[:, s]
                y4 = y_of[(block, g)]
                nc.scalar.activation(
                    out=squares[e], in_=banks[e], func=ACT.Square, bias=bias[:, j : j + 1], scale=1.0
                )
                if gain_engines[e] == "V":
                    nc.vector.tensor_scalar(
                        out=y4[:, t, :],
                        in0=banks[e],
                        scalar1=gain[:, j : j + 1],
                        scalar2=gain_bias[:, j : j + 1],
                        op0=ALU.mult,
                        op1=ALU.add,
                    )
                else:
                    nc.scalar.activation(
                        out=y4[:, t, :],
                        in_=banks[e],
                        func=ACT.Identity,
                        bias=gain_bias[:, j : j + 1],
                        scale=gain[:, j : j + 1],
                    )
                if j > 0 and (wide or (e == 1 and m > 0)):
                    acc = acc_of[block]
                    nc.vector.tensor_tensor(out=acc[:], in0=acc[:], in1=sq[:] if not wide else squares[e], op=ALU.add)

        def rms_factor(block):
            n = BLOCKS[block][1]
            bank = psum.tile([P, BATCH], F32, name="mm")
            for h in range(BATCH // n):
                nc.tensor.matmul(
                    out=bank[:, 0:n],
                    lhsT=mean_w[:],
                    rhs=acc_of[block][:, h * n : (h + 1) * n],
                    start=(h == 0),
                    stop=(h == BATCH // n - 1),
                )
            inv = norm_pool.tile([P, BATCH], F32, name="inv")
            nc.scalar.activation(
                out=inv[:, 0:n], in_=bank[:, 0:n], func=ACT.Abs_reciprocal_sqrt, bias=eps[:, 0:1], scale=1.0
            )
            inv_of[block] = inv

        q_grouped_of = {}

        def normalise(block, g):
            n = BLOCKS[block][1]
            q_grouped = q_pool.tile([P, 4 * BATCH], BF16, name="q_grouped", align_bytes=64)
            nc.vector.tensor_tensor(
                out=q_grouped[:, 0 : 4 * n].rearrange("p (c i t) -> p c t i", i=4, t=4),
                in0=y_of[(block, g)].rearrange("p t (c i) -> p c t i", i=4),
                in1=inv_of[block][:, 0:n]
                .rearrange("p (c i) -> p c i", i=4)
                .unsqueeze(2)
                .to_broadcast([P, n // 4, 4, 4]),
                op=ALU.mult,
            )
            q_grouped_of[(block, g)] = q_grouped

        def quantise_q(block, g):
            first, n = BLOCKS[block]
            q_codes, q_scales = operand("q", first // BATCH)
            tokens = slice(first % BATCH, first % BATCH + n)
            nc.vector.quantize_mx(
                out=q_codes[:, g, tokens].bitcast(FP8X4),
                scales=q_scales[:, g, tokens],
                in_=q_grouped_of[(block, g)][:, 0 : 4 * n],
            )

        score_of = {}

        def score(block, parts, tag):
            first, n = BLOCKS[block]
            batch = first // BATCH
            q_codes, q_scales = operand("q", batch)

            def multiply_keys(out, i, h, g):
                key_codes, key_scales = unit_operand_of[("keys", 2 * batch + h)]
                tokens = slice(first % BATCH + i * P, first % BATCH + (i + 1) * P)
                rows = slice(g * UNIT_ROWS, (g + 1) * UNIT_ROWS)
                nc.tensor.matmul_mx(
                    out=out,
                    lhsT=q_codes[:, g, tokens].bitcast(FP8X4),
                    lhsT_scale=q_scales[:, g, tokens],
                    rhs=key_codes[:, rows].bitcast(FP8X4),
                    rhs_scale=key_scales[:, rows],
                    start=(g == 0),
                    stop=(g == PASSES - 1),
                )

            banks = []
            for p in range(len(parts)):
                bank = psum.tile([P, BATCH], F32, name="sc%d_%d" % (block, len(score_of) + p), tag=tag)
                banks.append(bank)
            if len(parts[0]) == 2:
                for bank, part in zip(banks, parts):
                    for x in range(2):
                        for g in range(PASSES):
                            i, h = part[x]
                            multiply_keys(bank[:, x * UNIT_ROWS : (x + 1) * UNIT_ROWS], i, h, g)
            else:
                for g in range(PASSES):
                    for bank, part in zip(banks, parts):
                        i, h = part[0]
                        multiply_keys(bank[:, 0:UNIT_ROWS], i, h, g)
            for bank, part in zip(banks, parts):
                score_of[(block, part)] = bank

        def store_scores(block, parts, copy_engines):
            first, n = BLOCKS[block]
            for part, engine in zip(parts, copy_engines):
                bank = score_of[(block, part)]
                width = len(part) * UNIT_ROWS
                i, h = part[0]
                o_sb = o_pool.tile([P, BATCH], F32, name="o_sb")
                if engine == "V":
                    nc.vector.tensor_scalar_mul(out=o_sb[:, 0:width], in0=bank[:, 0:width], scalar1=SCORE_SCALE)
                else:
                    nc.scalar.activation(
                        out=o_sb[:, 0:width], in_=bank[:, 0:width], func=ACT.Copy, scale=SCORE_SCALE
                    )
                rows = slice(first + i * P, first + (i + 1) * P)
                nc.sync.dma_start(
                    out=out_rows[rows, h * UNIT_ROWS : h * UNIT_ROWS + width], in_=o_sb[:, 0:width]
                )

        whole = [((i, 0), (i, 1)) for i in range(4)]
        single = [((i, h),) for i in range(2) for h in range(2)]

        next_unit = 0
        for n in range(LEAD + 1):
            prepare(n)
            if n == 1:
                spread_bias_and_gain()
        next_unit = LEAD + 1
        for m in range(W_UNITS):
            if next_unit < 12:
                prepare(next_unit)
                next_unit += 1
            project(0, m, "VS")

        prepare(next_unit)
        next_unit += 1
        for m in range(W_UNITS):
            project(1, m, "SS")
            if m == 0:
                rms_factor(0)
            if m == 4:
                prepare(next_unit)
                next_unit += 1
            if m % 2 == 1:
                normalise(0, m // 2)
            elif m > 0:
                quantise_q(0, m // 2 - 1)

        for m in range(W_UNITS - 1):
            project(2, m, "SS")
            if m == 0:
                quantise_q(0, 3)
                rms_factor(1)
            if m in (2, 5):
                prepare(next_unit)
                next_unit += 1
            if m % 2 == 1:
                normalise(1, m // 2)
            elif m > 0:
                quantise_q(1, m // 2 - 1)

        ctx.enter_context(tc.manual_schedule())
        project(2, W_UNITS - 1, "SS")
        score(0, whole[0:2], "tp")
        rms_factor(2)
        normalise(1, 3)
        quantise_q(1, 3)
        score(0, whole[2:4], "tp")
        store_scores(0, whole, "SSSS")
        score(1, whole[0:2], "mm")
        store_scores(1, whole[0:2], "SS")
        for g in range(PASSES):
            normalise(2, g)
            if g > 0:
                quantise_q(2, g - 1)
        quantise_q(2, 3)
        score(2, single, "mm")
        store_scores(2, single, "SVSV")
